import numpy as np
import ml_dtypes


def mxq(x, axis, fmt="e4m3"):
    dtype, down = {"e4m3": (ml_dtypes.float8_e4m3fn, 7), "e5m2": (ml_dtypes.float8_e5m2, 14)}[fmt]
    v = np.moveaxis(np.asarray(x, np.float32).astype(ml_dtypes.bfloat16).astype(np.float64), axis, -1)
    blocks = v.reshape(v.shape[:-1] + (-1, 32))
    amax = np.abs(blocks).max(-1, keepdims=True)
    byte = np.maximum(np.where(amax > 0, np.frexp(amax)[1] - 1 + 127, 0) - down, 1)
    scale = np.exp2(byte - 127.0)
    codes = (blocks / scale).astype(np.float32).astype(dtype).astype(np.float64)
    return np.moveaxis((codes * scale).reshape(v.shape), -1, axis)


WIDE = False


def mx_kscale(k):
    if not WIDE:
        return np.ones(k)
    levels = np.array([10, -10, 5, -5, 0])
    a = np.random.permutation(np.resize(levels, k // 512 * 4)).reshape(k // 512, 4)
    idx = np.arange(k)
    return np.exp2(a[idx // 512, idx % 128 // 32])


BF16 = ml_dtypes.bfloat16


def bf(x):
    return np.asarray(x, np.float32).astype(BF16)


def f64(x):
    return np.asarray(x).astype(np.float64)


B, N, E, F, H, K, C, G, DEG = 8, 512, 4096, 32, 64, 8, 16, 64, 8


def incidence(rows, cols):
    return (np.random.uniform(size=(rows, cols)) < DEG / N) * np.random.uniform(0.5, 1.5, (rows, cols))


def setup_inputs():
    s, t = mx_kscale(N), mx_kscale(E)
    return {"x": bf(np.random.standard_normal((B, N, C)) / s[None, :, None]),
            "rinc": bf(incidence(E, N) * s[None, :]),
            "linc": bf(incidence(N, E) * t[None, :]),
            "edge_w": bf(np.random.standard_normal((E, K)) * 0.25 / t[:, None])}


def reference(x, rinc, linc, edge_w):
    z = mxq(f64(rinc), 1, "e4m3") @ mxq(f64(x), 1, "e4m3")
    m = (z[:, :, :, None] * f64(edge_w)[None, :, None, :]).reshape(B, E, C * K)
    return mxq(f64(linc), 1, "e4m3") @ mxq(m, 1, "e4m3")

@@ -1,0 +1,193 @@
+from contextlib import ExitStack
+
+import concourse.mybir as mybir
+from concourse.masks import make_identity
+
+F32 = mybir.dt.float32
+BF16 = mybir.dt.bfloat16
+U32 = mybir.dt.uint32
+U8 = mybir.dt.uint8
+FP8X4 = mybir.dt.float8_e4m3fn_x4
+
+P = 128
+PACK = 4
+K_PASS = P * PACK
+
+SIGNALS, NODES, EDGES, CHANNELS, KERNELS = 8, 512, 4096, 16, 8
+PASSES = EDGES // K_PASS
+NODE_TILES = NODES // P
+ROUNDS = 2
+UNITS = ROUNDS * PASSES
+Z_COLS = SIGNALS * CHANNELS // ROUNDS
+M_COLS = Z_COLS * KERNELS
+WORDS = P
+
+FLOPS = 2 * SIGNALS * EDGES * NODES * CHANNELS + 2 * SIGNALS * NODES * EDGES * CHANNELS * KERNELS
+
+
+def due(index, count):
+    return 0 <= index < count
+
+
+def tile_sgcn_pa_kernel(tc, x, rinc, linc, edge_w, out):
+    nc = tc.nc
+    with ExitStack() as stack:
+        keep = stack.enter_context(tc.tile_pool(name="keep", bufs=1))
+        stage = stack.enter_context(tc.tile_pool(name="stage", bufs=2))
+        results = stack.enter_context(tc.tile_pool(name="results", bufs=NODE_TILES))
+        turn_banks = stack.enter_context(tc.psum_pool(name="turn_banks", bufs=2))
+        z_banks = stack.enter_context(tc.psum_pool(name="z_banks", bufs=2))
+        y_banks = stack.enter_context(tc.psum_pool(name="y_banks", bufs=1))
+        stack.enter_context(tc.manual_schedule())
+
+        x_raw = keep.tile([P, SIGNALS, PACK, CHANNELS], BF16)
+        for u in range(2):
+            nc.scalar.dma_start(
+                out=x_raw[:, :, 2 * u : 2 * u + 2, :].rearrange("q b h c -> q b (h c)"),
+                in_=x[:, 256 * u : 256 * (u + 1), :].rearrange("b (q h) c -> q b (h c)", h=2),
+            )
+        w_raw = keep.tile([P, PASSES * PACK * KERNELS], BF16)
+        nc.scalar.dma_start(
+            out=w_raw[:].rearrange("p (j hk) -> p j hk", hk=2 * KERNELS),
+            in_=edge_w.rearrange("(j p h) k -> p j (h k)", p=P, h=2),
+        )
+        rinc_raw = []
+        linc_raw = []
+        for g in range(PASSES):
+            edges = slice(K_PASS * g, K_PASS * (g + 1))
+            rows = keep.tile([P, PACK * NODES], BF16, name="rinc_raw%d" % g)
+            nc.sync.dma_start(
+                out=rows[:].rearrange("p (u hn) -> p u hn", u=2),
+                in_=rinc[edges, :].rearrange("(u p h) n -> p u (h n)", u=2, h=2),
+            )
+            rinc_raw.append(rows)
+            cols = keep.tile([P, NODE_TILES * K_PASS], BF16, name="linc_raw%d" % g)
+            nc.sync.dma_start(
+                out=cols[:].rearrange("p (i e) -> p i e", i=NODE_TILES),
+                in_=linc[:, edges].rearrange("(i p) e -> p i e", p=P),
+            )
+            linc_raw.append(cols)
+
+        ident = keep.tile([P, P], F32)
+        make_identity(nc, ident[:])
+
+        x_codes = keep.tile([P, SIGNALS * CHANNELS], U32, align_bytes=64)
+        x_scales = keep.tile([P, SIGNALS * CHANNELS], U8, align_bytes=64)
+        rinc_codes = keep.tile([P, PASSES, K_PASS], U32, align_bytes=64)
+        rinc_scales = keep.tile([P, PASSES, K_PASS], U8, align_bytes=64)
+        linc_codes = keep.tile([P, PASSES, NODES], U32, align_bytes=64)
+        linc_scales = keep.tile([P, PASSES, NODES], U8, align_bytes=64)
+
+        x_grouped = keep.tile([P, SIGNALS * CHANNELS * PACK], BF16, align_bytes=64)
+        nc.vector.tensor_copy(
+            out=x_grouped[:].rearrange("q (b c s) -> q b c s", b=SIGNALS, s=PACK),
+            in_=x_raw[:].rearrange("q b s c -> q b c s"),
+        )
+        nc.vector.quantize_mx(out=x_codes[:].bitcast(FP8X4), scales=x_scales[:], in_=x_grouped[:])
+
+        grouped = {}
+        z = {}
+        m_codes = {}
+        m_scales = {}
+        y_acc = {}
+
+        def turn(name, g, raw):
+            raw_words = raw[:].bitcast(F32).rearrange("p (a u w) -> p a u w", a=4, u=2)
+            tile = stage.tile([P, PACK * K_PASS], BF16, name=name, align_bytes=64)
+            tile_words = tile[:].bitcast(F32).rearrange("p (a r u) -> p a r u", a=4, u=2)
+            for pair in range(2):
+                bank = turn_banks.tile([P, 2, 2, WORDS], F32)
+                for a in range(2):
+                    for u in range(2):
+                        nc.tensor.transpose(bank[:, a, u, :], raw_words[:, 2 * pair + a, u, :], ident[:])
+                nc.scalar.copy(
+                    out=tile_words[:, 2 * pair : 2 * pair + 2],
+                    in_=bank[:].rearrange("p a u r -> p a r u"),
+                )
+            grouped[name, g] = tile
+
+        def quantise(name, g, codes, scales):
+            nc.vector.quantize_mx(out=codes.bitcast(FP8X4), scales=scales, in_=grouped[name, g][:])
+
+        def first_matmul(unit):
+            r, g = divmod(unit, PASSES)
+            cols = slice(Z_COLS * r, Z_COLS * (r + 1))
+            z[unit] = z_banks.tile([P, PACK, Z_COLS], F32, name="z")
+            for t in range(PACK):
+                rows = slice(P * t, P * (t + 1))
+                nc.tensor.matmul_mx(
+                    out=z[unit][:, t, :],
+                    lhsT=rinc_codes[:, g, rows].bitcast(FP8X4),
+                    lhsT_scale=rinc_scales[:, g, rows],
+                    rhs=x_codes[:, cols].bitcast(FP8X4),
+                    rhs_scale=x_scales[:, cols],
+                    start=True,
+                    stop=True,
+                )
+
+        def messages(unit):
+            g = unit % PASSES
+            w_g = w_raw[:, PACK * KERNELS * g : PACK * KERNELS * (g + 1)].rearrange("p (t k) -> p k t", k=KERNELS)
+            shape = [P, KERNELS, Z_COLS, PACK]
+            tile = stage.tile([P, M_COLS * PACK], BF16, name="m_grouped", align_bytes=64)
+            nc.vector.tensor_tensor(
+                out=tile[:].rearrange("p (k c t) -> p k c t", k=KERNELS, t=PACK),
+                in0=z[unit][:].rearrange("p t c -> p c t").unsqueeze(1).to_broadcast(shape),
+                in1=w_g.unsqueeze(2).to_broadcast(shape),
+                op=mybir.AluOpType.mult,
+            )
+            grouped["m", unit] = tile
+
+        def second_matmul(unit):
+            r, g = divmod(unit, PASSES)
+            for i in range(NODE_TILES):
+                if g == 0:
+                    y_acc[i] = y_banks.tile([P, M_COLS], F32, name="y_acc%d" % i)
+                nodes = slice(P * i, P * (i + 1))
+                nc.tensor.matmul_mx(
+                    out=y_acc[i][:],
+                    lhsT=linc_codes[:, g, nodes].bitcast(FP8X4),
+                    lhsT_scale=linc_scales[:, g, nodes],
+                    rhs=m_codes[unit][:].bitcast(FP8X4),
+                    rhs_scale=m_scales[unit][:],
+                    start=(g == 0),
+                    stop=(g == PASSES - 1),
+                )
+
+        def store_round(r):
+            per_round = SIGNALS // ROUNDS
+            for i in range(NODE_TILES):
+                y_sb = results.tile([P, M_COLS], F32)
+                if r == ROUNDS - 1 and i % 2 == 1:
+                    copy = nc.vector.tensor_copy
+                else:
+                    copy = nc.scalar.copy
+                copy(
+                    out=y_sb[:].rearrange("p (c k) -> p c k", k=KERNELS),
+                    in_=y_acc[i][:].rearrange("p (k c) -> p c k", k=KERNELS),
+                )
+                nc.sync.dma_start(
+                    out=out[per_round * r : per_round * (r + 1), P * i : P * (i + 1), :].rearrange("b p j -> p b j"),
+                    in_=y_sb[:].rearrange("p (b j) -> p b j", b=per_round),
+                )
+
+        for u in range(-2, UNITS + 1):
+            if due(u, UNITS):
+                messages(u)
+            if due(u + 1, PASSES):
+                quantise("rinc", u + 1, rinc_codes[:, u + 1, :], rinc_scales[:, u + 1, :])
+            if due(u + 1, UNITS):
+                first_matmul(u + 1)
+            if due(u + 2, PASSES):
+                turn("rinc", u + 2, rinc_raw[u + 2])
+            if due(u, PASSES):
+                quantise("linc", u, linc_codes[:, u, :], linc_scales[:, u, :])
+            if due(u - 1, UNITS):
+                m_codes[u - 1] = stage.tile([P, M_COLS], U32, name="m_codes", align_bytes=64)
+                m_scales[u - 1] = stage.tile([P, M_COLS], U8, name="m_scales", align_bytes=64)
+                quantise("m", u - 1, m_codes[u - 1][:], m_scales[u - 1][:])
+                second_matmul(u - 1)
+                if u % PASSES == 0:
+                    store_round((u - 1) // PASSES)
+            if due(u + 2, PASSES):
+                turn("linc", u + 2, linc_raw[u + 2])

@@ -21,6 +21,7 @@ UNITS = ROUNDS * PASSES
 Z_COLS = SIGNALS * CHANNELS // ROUNDS
 M_COLS = Z_COLS * KERNELS
 WORDS = P
+VECTOR_KERNELS = 6
 
 FLOPS = 2 * SIGNALS * EDGES * NODES * CHANNELS + 2 * SIGNALS * NODES * EDGES * CHANNELS * KERNELS
 
@@ -71,6 +72,12 @@ def tile_sgcn_pa_kernel(tc, x, rinc, linc, edge_w, out):
         ident = keep.tile([P, P], F32)
         make_identity(nc, ident[:])
 
+        w_grouped = keep.tile([P, PASSES, KERNELS, PACK], F32)
+        nc.vector.tensor_copy(
+            out=w_grouped[:],
+            in_=w_raw[:].rearrange("p (g t k) -> p g k t", g=PASSES, k=KERNELS),
+        )
+
         x_codes = keep.tile([P, SIGNALS * CHANNELS], U32, align_bytes=64)
         x_scales = keep.tile([P, SIGNALS * CHANNELS], U8, align_bytes=64)
         rinc_codes = keep.tile([P, PASSES, K_PASS], U32, align_bytes=64)
@@ -87,6 +94,7 @@ def tile_sgcn_pa_kernel(tc, x, rinc, linc, edge_w, out):
 
         grouped = {}
         z = {}
+        z_copy = {}
         m_codes = {}
         m_scales = {}
         y_acc = {}
@@ -124,16 +132,25 @@ def tile_sgcn_pa_kernel(tc, x, rinc, linc, edge_w, out):
                     start=True,
                     stop=True,
                 )
+            z_copy[unit] = stage.tile([P, Z_COLS, PACK], F32, name="z_copy")
+            nc.scalar.copy(out=z_copy[unit][:], in_=z[unit][:].rearrange("p t c -> p c t"))
 
         def messages(unit):
             g = unit % PASSES
-            w_g = w_raw[:, PACK * KERNELS * g : PACK * KERNELS * (g + 1)].rearrange("p (t k) -> p k t", k=KERNELS)
-            shape = [P, KERNELS, Z_COLS, PACK]
             tile = stage.tile([P, M_COLS * PACK], BF16, name="m_grouped", align_bytes=64)
+            planes = tile[:].rearrange("p (k c t) -> p k c t", k=KERNELS, t=PACK)
+            shape = [P, VECTOR_KERNELS, Z_COLS, PACK]
             nc.vector.tensor_tensor(
-                out=tile[:].rearrange("p (k c t) -> p k c t", k=KERNELS, t=PACK),
+                out=planes[:, :VECTOR_KERNELS],
                 in0=z[unit][:].rearrange("p t c -> p c t").unsqueeze(1).to_broadcast(shape),
-                in1=w_g.unsqueeze(2).to_broadcast(shape),
+                in1=w_grouped[:, g, :VECTOR_KERNELS, :].unsqueeze(2).to_broadcast(shape),
+                op=mybir.AluOpType.mult,
+            )
+            shape = [P, KERNELS - VECTOR_KERNELS, Z_COLS, PACK]
+            nc.gpsimd.tensor_tensor(
+                out=planes[:, VECTOR_KERNELS:],
+                in0=z_copy[unit][:].unsqueeze(1).to_broadcast(shape),
+                in1=w_grouped[:, g, VECTOR_KERNELS:, :].unsqueeze(2).to_broadcast(shape),
                 op=mybir.AluOpType.mult,
             )
             grouped["m", unit] = tile

@@ -34,10 +34,10 @@ def tile_sgcn_pa_kernel(tc, x, rinc, linc, edge_w, out):
     nc = tc.nc
     with ExitStack() as stack:
         keep = stack.enter_context(tc.tile_pool(name="keep", bufs=1))
+        turned = stack.enter_context(tc.tile_pool(name="turned", bufs=3))
         stage = stack.enter_context(tc.tile_pool(name="stage", bufs=2))
         results = stack.enter_context(tc.tile_pool(name="results", bufs=NODE_TILES))
-        turn_banks = stack.enter_context(tc.psum_pool(name="turn_banks", bufs=2))
-        z_banks = stack.enter_context(tc.psum_pool(name="z_banks", bufs=2))
+        work_banks = stack.enter_context(tc.psum_pool(name="work_banks", bufs=4))
         y_banks = stack.enter_context(tc.psum_pool(name="y_banks", bufs=1))
         stack.enter_context(tc.manual_schedule())
 
@@ -73,7 +73,7 @@ def tile_sgcn_pa_kernel(tc, x, rinc, linc, edge_w, out):
         make_identity(nc, ident[:])
 
         w_grouped = keep.tile([P, PASSES, KERNELS, PACK], F32)
-        nc.vector.tensor_copy(
+        nc.gpsimd.tensor_copy(
             out=w_grouped[:],
             in_=w_raw[:].rearrange("p (g t k) -> p g k t", g=PASSES, k=KERNELS),
         )
@@ -101,10 +101,10 @@ def tile_sgcn_pa_kernel(tc, x, rinc, linc, edge_w, out):
 
         def turn(name, g, raw):
             raw_words = raw[:].bitcast(F32).rearrange("p (a u w) -> p a u w", a=4, u=2)
-            tile = stage.tile([P, PACK * K_PASS], BF16, name=name, align_bytes=64)
+            tile = turned.tile([P, PACK * K_PASS], BF16, name=name, align_bytes=64)
             tile_words = tile[:].bitcast(F32).rearrange("p (a r u) -> p a r u", a=4, u=2)
             for pair in range(2):
-                bank = turn_banks.tile([P, 2, 2, WORDS], F32)
+                bank = work_banks.tile([P, 2, 2, WORDS], F32, tag="work")
                 for a in range(2):
                     for u in range(2):
                         nc.tensor.transpose(bank[:, a, u, :], raw_words[:, 2 * pair + a, u, :], ident[:])
@@ -120,7 +120,7 @@ def tile_sgcn_pa_kernel(tc, x, rinc, linc, edge_w, out):
         def first_matmul(unit):
             r, g = divmod(unit, PASSES)
             cols = slice(Z_COLS * r, Z_COLS * (r + 1))
-            z[unit] = z_banks.tile([P, PACK, Z_COLS], F32, name="z")
+            z[unit] = work_banks.tile([P, PACK, Z_COLS], F32, name="z", tag="work")
             for t in range(PACK):
                 rows = slice(P * t, P * (t + 1))
                 nc.tensor.matmul_mx(
@@ -188,17 +188,15 @@ def tile_sgcn_pa_kernel(tc, x, rinc, linc, edge_w, out):
                     in_=y_sb[:].rearrange("p (b j) -> p b j", b=per_round),
                 )
 
-        for u in range(-2, UNITS + 1):
+        for u in range(-3, UNITS + 1):
             if due(u, UNITS):
                 messages(u)
+            if due(u, PASSES):
+                quantise("linc", u, linc_codes[:, u, :], linc_scales[:, u, :])
             if due(u + 1, PASSES):
                 quantise("rinc", u + 1, rinc_codes[:, u + 1, :], rinc_scales[:, u + 1, :])
             if due(u + 1, UNITS):
                 first_matmul(u + 1)
-            if due(u + 2, PASSES):
-                turn("rinc", u + 2, rinc_raw[u + 2])
-            if due(u, PASSES):
-                quantise("linc", u, linc_codes[:, u, :], linc_scales[:, u, :])
             if due(u - 1, UNITS):
                 m_codes[u - 1] = stage.tile([P, M_COLS], U32, name="m_codes", align_bytes=64)
                 m_scales[u - 1] = stage.tile([P, M_COLS], U8, name="m_scales", align_bytes=64)
@@ -208,3 +206,5 @@ def tile_sgcn_pa_kernel(tc, x, rinc, linc, edge_w, out):
                     store_round((u - 1) // PASSES)
             if due(u + 2, PASSES):
                 turn("linc", u + 2, linc_raw[u + 2])
+            if due(u + 3, PASSES):
+                turn("rinc", u + 3, rinc_raw[u + 3])

@@ -21,7 +21,8 @@ UNITS = ROUNDS * PASSES
 Z_COLS = SIGNALS * CHANNELS // ROUNDS
 M_COLS = Z_COLS * KERNELS
 WORDS = P
-VECTOR_KERNELS = 6
+SCALAR_KERNELS_FIRST_ROUND = 1
+SCALAR_KERNELS_LATER = 2
 
 FLOPS = 2 * SIGNALS * EDGES * NODES * CHANNELS + 2 * SIGNALS * NODES * EDGES * CHANNELS * KERNELS
 
@@ -94,7 +95,6 @@ def tile_sgcn_pa_kernel(tc, x, rinc, linc, edge_w, out):
 
         grouped = {}
         z = {}
-        z_copy = {}
         m_codes = {}
         m_scales = {}
         y_acc = {}
@@ -132,27 +132,27 @@ def tile_sgcn_pa_kernel(tc, x, rinc, linc, edge_w, out):
                     start=True,
                     stop=True,
                 )
-            z_copy[unit] = stage.tile([P, Z_COLS, PACK], F32, name="z_copy")
-            nc.scalar.copy(out=z_copy[unit][:], in_=z[unit][:].rearrange("p t c -> p c t"))
 
         def messages(unit):
-            g = unit % PASSES
-            tile = stage.tile([P, M_COLS * PACK], BF16, name="m_grouped", align_bytes=64)
+            r, g = divmod(unit, PASSES)
+            vector_kernels = KERNELS - (SCALAR_KERNELS_FIRST_ROUND if r == 0 else SCALAR_KERNELS_LATER)
+            tile = turned.tile([P, M_COLS * PACK], BF16, name="m_grouped", align_bytes=64)
             planes = tile[:].rearrange("p (k c t) -> p k c t", k=KERNELS, t=PACK)
-            shape = [P, VECTOR_KERNELS, Z_COLS, PACK]
+            shape = [P, vector_kernels, Z_COLS, PACK]
             nc.vector.tensor_tensor(
-                out=planes[:, :VECTOR_KERNELS],
+                out=planes[:, :vector_kernels],
                 in0=z[unit][:].rearrange("p t c -> p c t").unsqueeze(1).to_broadcast(shape),
-                in1=w_grouped[:, g, :VECTOR_KERNELS, :].unsqueeze(2).to_broadcast(shape),
+                in1=w_grouped[:, g, :vector_kernels, :].unsqueeze(2).to_broadcast(shape),
                 op=mybir.AluOpType.mult,
             )
-            shape = [P, KERNELS - VECTOR_KERNELS, Z_COLS, PACK]
-            nc.gpsimd.tensor_tensor(
-                out=planes[:, VECTOR_KERNELS:],
-                in0=z_copy[unit][:].unsqueeze(1).to_broadcast(shape),
-                in1=w_grouped[:, g, VECTOR_KERNELS:, :].unsqueeze(2).to_broadcast(shape),
-                op=mybir.AluOpType.mult,
-            )
+            for k in range(vector_kernels, KERNELS):
+                for t in range(PACK):
+                    nc.scalar.activation(
+                        out=planes[:, k, :, t],
+                        in_=z[unit][:, t, :],
+                        func=mybir.ActivationFunctionType.Copy,
+                        scale=w_grouped[:, g, k, t : t + 1],
+                    )
             grouped["m", unit] = tile
 
         def second_matmul(unit):
@@ -188,15 +188,17 @@ def tile_sgcn_pa_kernel(tc, x, rinc, linc, edge_w, out):
                     in_=y_sb[:].rearrange("p (b j) -> p b j", b=per_round),
                 )
 
-        for u in range(-3, UNITS + 1):
+        for u in range(-2, UNITS + 1):
             if due(u, UNITS):
                 messages(u)
-            if due(u, PASSES):
-                quantise("linc", u, linc_codes[:, u, :], linc_scales[:, u, :])
             if due(u + 1, PASSES):
                 quantise("rinc", u + 1, rinc_codes[:, u + 1, :], rinc_scales[:, u + 1, :])
             if due(u + 1, UNITS):
                 first_matmul(u + 1)
+            if due(u + 2, PASSES):
+                turn("rinc", u + 2, rinc_raw[u + 2])
+            if due(u, PASSES):
+                quantise("linc", u, linc_codes[:, u, :], linc_scales[:, u, :])
             if due(u - 1, UNITS):
                 m_codes[u - 1] = stage.tile([P, M_COLS], U32, name="m_codes", align_bytes=64)
                 m_scales[u - 1] = stage.tile([P, M_COLS], U8, name="m_scales", align_bytes=64)
@@ -206,5 +208,3 @@ def tile_sgcn_pa_kernel(tc, x, rinc, linc, edge_w, out):
                     store_round((u - 1) // PASSES)
             if due(u + 2, PASSES):
                 turn("linc", u + 2, linc_raw[u + 2])
-            if due(u + 3, PASSES):
-                turn("rinc", u + 3, rinc_raw[u + 3])

@@ -23,6 +23,7 @@ M_COLS = Z_COLS * KERNELS
 WORDS = P
 SCALAR_KERNELS_FIRST_ROUND = 1
 SCALAR_KERNELS_LATER = 2
+RINC_LEAD = 2
 
 FLOPS = 2 * SIGNALS * EDGES * NODES * CHANNELS + 2 * SIGNALS * NODES * EDGES * CHANNELS * KERNELS
 
@@ -35,8 +36,7 @@ def tile_sgcn_pa_kernel(tc, x, rinc, linc, edge_w, out):
     nc = tc.nc
     with ExitStack() as stack:
         keep = stack.enter_context(tc.tile_pool(name="keep", bufs=1))
-        turned = stack.enter_context(tc.tile_pool(name="turned", bufs=3))
-        stage = stack.enter_context(tc.tile_pool(name="stage", bufs=2))
+        stage = stack.enter_context(tc.tile_pool(name="stage", bufs=3))
         results = stack.enter_context(tc.tile_pool(name="results", bufs=NODE_TILES))
         work_banks = stack.enter_context(tc.psum_pool(name="work_banks", bufs=4))
         y_banks = stack.enter_context(tc.psum_pool(name="y_banks", bufs=1))
@@ -55,20 +55,22 @@ def tile_sgcn_pa_kernel(tc, x, rinc, linc, edge_w, out):
         )
         rinc_raw = []
         linc_raw = []
-        for g in range(PASSES):
-            edges = slice(K_PASS * g, K_PASS * (g + 1))
-            rows = keep.tile([P, PACK * NODES], BF16, name="rinc_raw%d" % g)
-            nc.sync.dma_start(
-                out=rows[:].rearrange("p (u hn) -> p u hn", u=2),
-                in_=rinc[edges, :].rearrange("(u p h) n -> p u (h n)", u=2, h=2),
-            )
-            rinc_raw.append(rows)
-            cols = keep.tile([P, NODE_TILES * K_PASS], BF16, name="linc_raw%d" % g)
-            nc.sync.dma_start(
-                out=cols[:].rearrange("p (i e) -> p i e", i=NODE_TILES),
-                in_=linc[:, edges].rearrange("(i p) e -> p i e", p=P),
-            )
-            linc_raw.append(cols)
+        for step in range(PASSES + RINC_LEAD):
+            if step < PASSES:
+                rows = keep.tile([P, PACK * NODES], BF16, name="rinc_raw%d" % step)
+                nc.sync.dma_start(
+                    out=rows[:].rearrange("p (u hn) -> p u hn", u=2),
+                    in_=rinc[K_PASS * step : K_PASS * (step + 1), :].rearrange("(u p h) n -> p u (h n)", u=2, h=2),
+                )
+                rinc_raw.append(rows)
+            if step >= RINC_LEAD:
+                g = step - RINC_LEAD
+                cols = keep.tile([P, NODE_TILES * K_PASS], BF16, name="linc_raw%d" % g)
+                nc.sync.dma_start(
+                    out=cols[:].rearrange("p (i e) -> p i e", i=NODE_TILES),
+                    in_=linc[:, K_PASS * g : K_PASS * (g + 1)].rearrange("(i p) e -> p i e", p=P),
+                )
+                linc_raw.append(cols)
 
         ident = keep.tile([P, P], F32)
         make_identity(nc, ident[:])
@@ -101,7 +103,7 @@ def tile_sgcn_pa_kernel(tc, x, rinc, linc, edge_w, out):
 
         def turn(name, g, raw):
             raw_words = raw[:].bitcast(F32).rearrange("p (a u w) -> p a u w", a=4, u=2)
-            tile = turned.tile([P, PACK * K_PASS], BF16, name=name, align_bytes=64)
+            tile = stage.tile([P, PACK * K_PASS], BF16, name=name, align_bytes=64)
             tile_words = tile[:].bitcast(F32).rearrange("p (a r u) -> p a r u", a=4, u=2)
             for pair in range(2):
                 bank = work_banks.tile([P, 2, 2, WORDS], F32, tag="work")
@@ -136,7 +138,7 @@ def tile_sgcn_pa_kernel(tc, x, rinc, linc, edge_w, out):
         def messages(unit):
             r, g = divmod(unit, PASSES)
             vector_kernels = KERNELS - (SCALAR_KERNELS_FIRST_ROUND if r == 0 else SCALAR_KERNELS_LATER)
-            tile = turned.tile([P, M_COLS * PACK], BF16, name="m_grouped", align_bytes=64)
+            tile = stage.tile([P, M_COLS * PACK], BF16, name="m_grouped", align_bytes=64)
             planes = tile[:].rearrange("p (k c t) -> p k c t", k=KERNELS, t=PACK)
             shape = [P, vector_kernels, Z_COLS, PACK]
             nc.vector.tensor_tensor(
@@ -155,9 +157,9 @@ def tile_sgcn_pa_kernel(tc, x, rinc, linc, edge_w, out):
                     )
             grouped["m", unit] = tile
 
-        def second_matmul(unit):
-            r, g = divmod(unit, PASSES)
-            for i in range(NODE_TILES):
+        def second_matmul(unit, node_tiles):
+            g = unit % PASSES
+            for i in node_tiles:
                 if g == 0:
                     y_acc[i] = y_banks.tile([P, M_COLS], F32, name="y_acc%d" % i)
                 nodes = slice(P * i, P * (i + 1))
@@ -188,23 +190,28 @@ def tile_sgcn_pa_kernel(tc, x, rinc, linc, edge_w, out):
                     in_=y_sb[:].rearrange("p (b j) -> p b j", b=per_round),
                 )
 
-        for u in range(-2, UNITS + 1):
+        first_tiles = range(NODE_TILES // 2)
+        last_tiles = range(NODE_TILES // 2, NODE_TILES)
+        for u in range(-3, UNITS + 2):
             if due(u, UNITS):
                 messages(u)
-            if due(u + 1, PASSES):
-                quantise("rinc", u + 1, rinc_codes[:, u + 1, :], rinc_scales[:, u + 1, :])
             if due(u + 1, UNITS):
                 first_matmul(u + 1)
+            if due(u - 2, UNITS):
+                second_matmul(u - 2, first_tiles)
+            if due(u + 3, PASSES):
+                turn("rinc", u + 3, rinc_raw[u + 3])
             if due(u + 2, PASSES):
-                turn("rinc", u + 2, rinc_raw[u + 2])
+                quantise("rinc", u + 2, rinc_codes[:, u + 2, :], rinc_scales[:, u + 2, :])
             if due(u, PASSES):
                 quantise("linc", u, linc_codes[:, u, :], linc_scales[:, u, :])
+            if due(u - 2, UNITS):
+                second_matmul(u - 2, last_tiles)
+                if (u - 2) % PASSES == PASSES - 1:
+                    store_round((u - 2) // PASSES)
+            if due(u + 1, PASSES):
+                turn("linc", u + 1, linc_raw[u + 1])
             if due(u - 1, UNITS):
                 m_codes[u - 1] = stage.tile([P, M_COLS], U32, name="m_codes", align_bytes=64)
                 m_scales[u - 1] = stage.tile([P, M_COLS], U8, name="m_scales", align_bytes=64)
                 quantise("m", u - 1, m_codes[u - 1][:], m_scales[u - 1][:])
-                second_matmul(u - 1)
-                if u % PASSES == 0:
-                    store_round((u - 1) // PASSES)
-            if due(u + 2, PASSES):
-                turn("linc", u + 2, linc_raw[u + 2])

@@ -40,7 +40,6 @@ def tile_sgcn_pa_kernel(tc, x, rinc, linc, edge_w, out):
         results = stack.enter_context(tc.tile_pool(name="results", bufs=NODE_TILES))
         work_banks = stack.enter_context(tc.psum_pool(name="work_banks", bufs=4))
         y_banks = stack.enter_context(tc.psum_pool(name="y_banks", bufs=1))
-        stack.enter_context(tc.manual_schedule())
 
         x_raw = keep.tile([P, SIGNALS, PACK, CHANNELS], BF16)
         for u in range(2):

@@ -40,6 +40,7 @@ def tile_sgcn_pa_kernel(tc, x, rinc, linc, edge_w, out):
         results = stack.enter_context(tc.tile_pool(name="results", bufs=NODE_TILES))
         work_banks = stack.enter_context(tc.psum_pool(name="work_banks", bufs=4))
         y_banks = stack.enter_context(tc.psum_pool(name="y_banks", bufs=1))
+        stack.enter_context(tc.manual_schedule())
 
         x_raw = keep.tile([P, SIGNALS, PACK, CHANNELS], BF16)
         for u in range(2):
@@ -176,10 +177,7 @@ def tile_sgcn_pa_kernel(tc, x, rinc, linc, edge_w, out):
             per_round = SIGNALS // ROUNDS
             for i in range(NODE_TILES):
                 y_sb = results.tile([P, M_COLS], F32)
-                if r == ROUNDS - 1 and i % 2 == 1:
-                    copy = nc.vector.tensor_copy
-                else:
-                    copy = nc.scalar.copy
+                copy = nc.scalar.copy if i % 2 == 0 else nc.vector.tensor_copy
                 copy(
                     out=y_sb[:].rearrange("p (c k) -> p c k", k=KERNELS),
                     in_=y_acc[i][:].rearrange("p (k c) -> p c k", k=KERNELS),

from contextlib import ExitStack

import concourse.mybir as mybir
from concourse.masks import make_identity

F32 = mybir.dt.float32
BF16 = mybir.dt.bfloat16
U32 = mybir.dt.uint32
U8 = mybir.dt.uint8
FP8X4 = mybir.dt.float8_e4m3fn_x4

P = 128
PACK = 4
K_PASS = P * PACK

SIGNALS, NODES, EDGES, CHANNELS, KERNELS = 8, 512, 4096, 16, 8
PASSES = EDGES // K_PASS
NODE_TILES = NODES // P
ROUNDS = 2
UNITS = ROUNDS * PASSES
Z_COLS = SIGNALS * CHANNELS // ROUNDS
M_COLS = Z_COLS * KERNELS
WORDS = P
SCALAR_KERNELS_FIRST_ROUND = 1
SCALAR_KERNELS_LATER = 2
RINC_LEAD = 2

FLOPS = 2 * SIGNALS * EDGES * NODES * CHANNELS + 2 * SIGNALS * NODES * EDGES * CHANNELS * KERNELS


def due(index, count):
    return 0 <= index < count


def tile_sgcn_pa_kernel(tc, x, rinc, linc, edge_w, out):
    nc = tc.nc
    with ExitStack() as stack:
        keep = stack.enter_context(tc.tile_pool(name="keep", bufs=1))
        stage = stack.enter_context(tc.tile_pool(name="stage", bufs=3))
        results = stack.enter_context(tc.tile_pool(name="results", bufs=NODE_TILES))
        work_banks = stack.enter_context(tc.psum_pool(name="work_banks", bufs=4))
        y_banks = stack.enter_context(tc.psum_pool(name="y_banks", bufs=1))
        stack.enter_context(tc.manual_schedule())

        x_raw = keep.tile([P, SIGNALS, PACK, CHANNELS], BF16)
        for u in range(2):
            nc.scalar.dma_start(
                out=x_raw[:, :, 2 * u : 2 * u + 2, :].rearrange("q b h c -> q b (h c)"),
                in_=x[:, 256 * u : 256 * (u + 1), :].rearrange("b (q h) c -> q b (h c)", h=2),
            )
        w_raw = keep.tile([P, PASSES * PACK * KERNELS], BF16)
        nc.scalar.dma_start(
            out=w_raw[:].rearrange("p (j hk) -> p j hk", hk=2 * KERNELS),
            in_=edge_w.rearrange("(j p h) k -> p j (h k)", p=P, h=2),
        )
        rinc_raw = []
        linc_raw = []
        for step in range(PASSES + RINC_LEAD):
            if step < PASSES:
                rows = keep.tile([P, PACK * NODES], BF16, name="rinc_raw%d" % step)
                nc.sync.dma_start(
                    out=rows[:].rearrange("p (u hn) -> p u hn", u=2),
                    in_=rinc[K_PASS * step : K_PASS * (step + 1), :].rearrange("(u p h) n -> p u (h n)", u=2, h=2),
                )
                rinc_raw.append(rows)
            if step >= RINC_LEAD:
                g = step - RINC_LEAD
                cols = keep.tile([P, NODE_TILES * K_PASS], BF16, name="linc_raw%d" % g)
                nc.sync.dma_start(
                    out=cols[:].rearrange("p (i e) -> p i e", i=NODE_TILES),
                    in_=linc[:, K_PASS * g : K_PASS * (g + 1)].rearrange("(i p) e -> p i e", p=P),
                )
                linc_raw.append(cols)

        ident = keep.tile([P, P], F32)
        make_identity(nc, ident[:])

        w_grouped = keep.tile([P, PASSES, KERNELS, PACK], F32)
        nc.gpsimd.tensor_copy(
            out=w_grouped[:],
            in_=w_raw[:].rearrange("p (g t k) -> p g k t", g=PASSES, k=KERNELS),
        )

        x_codes = keep.tile([P, SIGNALS * CHANNELS], U32, align_bytes=64)
        x_scales = keep.tile([P, SIGNALS * CHANNELS], U8, align_bytes=64)
        rinc_codes = keep.tile([P, PASSES, K_PASS], U32, align_bytes=64)
        rinc_scales = keep.tile([P, PASSES, K_PASS], U8, align_bytes=64)
        linc_codes = keep.tile([P, PASSES, NODES], U32, align_bytes=64)
        linc_scales = keep.tile([P, PASSES, NODES], U8, align_bytes=64)

        x_grouped = keep.tile([P, SIGNALS * CHANNELS * PACK], BF16, align_bytes=64)
        nc.vector.tensor_copy(
            out=x_grouped[:].rearrange("q (b c s) -> q b c s", b=SIGNALS, s=PACK),
            in_=x_raw[:].rearrange("q b s c -> q b c s"),
        )
        nc.vector.quantize_mx(out=x_codes[:].bitcast(FP8X4), scales=x_scales[:], in_=x_grouped[:])

        grouped = {}
        z = {}
        m_codes = {}
        m_scales = {}
        y_acc = {}

        def turn(name, g, raw):
            raw_words = raw[:].bitcast(F32).rearrange("p (a u w) -> p a u w", a=4, u=2)
            tile = stage.tile([P, PACK * K_PASS], BF16, name=name, align_bytes=64)
            tile_words = tile[:].bitcast(F32).rearrange("p (a r u) -> p a r u", a=4, u=2)
            for pair in range(2):
                bank = work_banks.tile([P, 2, 2, WORDS], F32, tag="work")
                for a in range(2):
                    for u in range(2):
                        nc.tensor.transpose(bank[:, a, u, :], raw_words[:, 2 * pair + a, u, :], ident[:])
                nc.scalar.copy(
                    out=tile_words[:, 2 * pair : 2 * pair + 2],
                    in_=bank[:].rearrange("p a u r -> p a r u"),
                )
            grouped[name, g] = tile

        def quantise(name, g, codes, scales):
            nc.vector.quantize_mx(out=codes.bitcast(FP8X4), scales=scales, in_=grouped[name, g][:])

        def first_matmul(unit):
            r, g = divmod(unit, PASSES)
            cols = slice(Z_COLS * r, Z_COLS * (r + 1))
            z[unit] = work_banks.tile([P, PACK, Z_COLS], F32, name="z", tag="work")
            for t in range(PACK):
                rows = slice(P * t, P * (t + 1))
                nc.tensor.matmul_mx(
                    out=z[unit][:, t, :],
                    lhsT=rinc_codes[:, g, rows].bitcast(FP8X4),
                    lhsT_scale=rinc_scales[:, g, rows],
                    rhs=x_codes[:, cols].bitcast(FP8X4),
                    rhs_scale=x_scales[:, cols],
                    start=True,
                    stop=True,
                )

        def messages(unit):
            r, g = divmod(unit, PASSES)
            vector_kernels = KERNELS - (SCALAR_KERNELS_FIRST_ROUND if r == 0 else SCALAR_KERNELS_LATER)
            tile = stage.tile([P, M_COLS * PACK], BF16, name="m_grouped", align_bytes=64)
            planes = tile[:].rearrange("p (k c t) -> p k c t", k=KERNELS, t=PACK)
            shape = [P, vector_kernels, Z_COLS, PACK]
            nc.vector.tensor_tensor(
                out=planes[:, :vector_kernels],
                in0=z[unit][:].rearrange("p t c -> p c t").unsqueeze(1).to_broadcast(shape),
                in1=w_grouped[:, g, :vector_kernels, :].unsqueeze(2).to_broadcast(shape),
                op=mybir.AluOpType.mult,
            )
            for k in range(vector_kernels, KERNELS):
                for t in range(PACK):
                    nc.scalar.activation(
                        out=planes[:, k, :, t],
                        in_=z[unit][:, t, :],
                        func=mybir.ActivationFunctionType.Copy,
                        scale=w_grouped[:, g, k, t : t + 1],
                    )
            grouped["m", unit] = tile

        def second_matmul(unit, node_tiles):
            g = unit % PASSES
            for i in node_tiles:
                if g == 0:
                    y_acc[i] = y_banks.tile([P, M_COLS], F32, name="y_acc%d" % i)
                nodes = slice(P * i, P * (i + 1))
                nc.tensor.matmul_mx(
                    out=y_acc[i][:],
                    lhsT=linc_codes[:, g, nodes].bitcast(FP8X4),
                    lhsT_scale=linc_scales[:, g, nodes],
                    rhs=m_codes[unit][:].bitcast(FP8X4),
                    rhs_scale=m_scales[unit][:],
                    start=(g == 0),
                    stop=(g == PASSES - 1),
                )

        def store_round(r):
            per_round = SIGNALS // ROUNDS
            for i in range(NODE_TILES):
                y_sb = results.tile([P, M_COLS], F32)
                copy = nc.scalar.copy if i % 2 == 0 else nc.vector.tensor_copy
                copy(
                    out=y_sb[:].rearrange("p (c k) -> p c k", k=KERNELS),
                    in_=y_acc[i][:].rearrange("p (k c) -> p c k", k=KERNELS),
                )
                nc.sync.dma_start(
                    out=out[per_round * r : per_round * (r + 1), P * i : P * (i + 1), :].rearrange("b p j -> p b j"),
                    in_=y_sb[:].rearrange("p (b j) -> p b j", b=per_round),
                )

        first_tiles = range(NODE_TILES // 2)
        last_tiles = range(NODE_TILES // 2, NODE_TILES)
        for u in range(-3, UNITS + 2):
            if due(u, UNITS):
                messages(u)
            if due(u + 1, UNITS):
                first_matmul(u + 1)
            if due(u - 2, UNITS):
                second_matmul(u - 2, first_tiles)
            if due(u + 3, PASSES):
                turn("rinc", u + 3, rinc_raw[u + 3])
            if due(u + 2, PASSES):
                quantise("rinc", u + 2, rinc_codes[:, u + 2, :], rinc_scales[:, u + 2, :])
            if due(u, PASSES):
                quantise("linc", u, linc_codes[:, u, :], linc_scales[:, u, :])
            if due(u - 2, UNITS):
                second_matmul(u - 2, last_tiles)
                if (u - 2) % PASSES == PASSES - 1:
                    store_round((u - 2) // PASSES)
            if due(u + 1, PASSES):
                turn("linc", u + 1, linc_raw[u + 1])
            if due(u - 1, UNITS):
                m_codes[u - 1] = stage.tile([P, M_COLS], U32, name="m_codes", align_bytes=64)
                m_scales[u - 1] = stage.tile([P, M_COLS], U8, name="m_scales", align_bytes=64)
                quantise("m", u - 1, m_codes[u - 1][:], m_scales[u - 1][:])
